import numpy as np
import ml_dtypes


def mxq(x, axis, fmt="e4m3"):
    dtype, down = {"e4m3": (ml_dtypes.float8_e4m3fn, 7), "e5m2": (ml_dtypes.float8_e5m2, 14)}[fmt]
    v = np.moveaxis(np.asarray(x, np.float32).astype(ml_dtypes.bfloat16).astype(np.float64), axis, -1)
    blocks = v.reshape(v.shape[:-1] + (-1, 32))
    amax = np.abs(blocks).max(-1, keepdims=True)
    byte = np.maximum(np.where(amax > 0, np.frexp(amax)[1] - 1 + 127, 0) - down, 1)
    scale = np.exp2(byte - 127.0)
    codes = (blocks / scale).astype(np.float32).astype(dtype).astype(np.float64)
    return np.moveaxis((codes * scale).reshape(v.shape), -1, axis)


WIDE = False


def mx_kscale(k):
    if not WIDE:
        return np.ones(k)
    levels = np.array([10, -10, 5, -5, 0])
    if k % 512:
        return np.exp2(np.random.permutation(np.resize(levels, k // 32))).repeat(32)
    a = np.empty((k // 512, 16))
    for p in range(k // 512):
        a[p, :8] = np.random.permutation(np.resize(levels, 8))
        for g in range(8):
            far = levels[np.abs(levels - a[p, g]) >= 10]
            a[p, g + 8] = far[np.random.randint(len(far))]
    return np.exp2(a.ravel()).repeat(32)


BF16 = ml_dtypes.bfloat16


def bf(x):
    return np.asarray(x, np.float32).astype(BF16)


def f64(x):
    return np.asarray(x).astype(np.float64)


E2M1 = np.array([0.0, 0.5, 1.0, 1.5, 2.0, 3.0, 4.0, 6.0, -0.0, -0.5, -1.0, -1.5, -2.0, -3.0, -4.0, -6.0])


def pack_weight(w, fmt):
    k, n = w.shape
    w = f64(bf(w)).reshape(k // 32, 32, n)
    amax = np.abs(w).max(1)
    if fmt == "e4m3":
        byte = np.frexp(amax)[1] - 1 + 127 - 7
    else:
        mant, ex = np.frexp(amax / 6.0)
        byte = np.where(mant > 0.5, ex, ex - 1) + 127
    byte = np.clip(np.where(amax > 0, byte, 1), 1, 254)
    scaled = (w * np.exp2(127.0 - byte)[:, None, :]).reshape(k, n).astype(np.float32)
    by_word = np.ascontiguousarray(scaled.reshape(k // 512, 128, 4, n).transpose(0, 1, 3, 2))
    if fmt == "e4m3":
        words = by_word.astype(ml_dtypes.float8_e4m3fn).view(np.uint8)
    else:
        c = by_word.astype(ml_dtypes.float4_e2m1fn).view(np.uint8) & 0xF
        words = c[..., 0::2] | (c[..., 1::2] << 4)
    return np.ascontiguousarray(words), np.ascontiguousarray(byte.astype(np.uint8).reshape(k // 512, 16, n))


def unpack_weight(words, scales, fmt):
    g, p, n, _ = words.shape
    if fmt == "e4m3":
        vals = np.ascontiguousarray(words).view(ml_dtypes.float8_e4m3fn).astype(np.float64)
    else:
        nib = np.empty((g, p, n, 4), np.uint8)
        nib[..., 0::2] = words & 0xF
        nib[..., 1::2] = words >> 4
        vals = E2M1[nib]
    vals = vals * np.repeat(np.exp2(scales.astype(np.float64) - 127.0), 8, axis=1)[..., None]
    return vals.transpose(0, 1, 3, 2).reshape(g * 512, n)
def pack4(w):
    words, scales = pack_weight(w, "e2m1")
    return words.reshape(words.shape[0], 128, -1), scales


def unpack4(words, scales):
    return unpack_weight(words.reshape(words.shape[0], 128, -1, 2), scales, "e2m1")


B, S, DIM, HDIM = 2, 256, 1024, 4096


def draw0():
    s = mx_kscale(DIM)
    t = np.exp2(np.round(np.log2(mx_kscale(HDIM)) / 2))
    x = bf(np.random.standard_normal((B, S, DIM)) * s)
    W1_words, W1_scales = pack4((np.random.standard_normal((HDIM, DIM)) * (1.0 / np.sqrt(DIM)) / s[None, :] * t[:, None]).T)
    W2_words, W2_scales = pack4(np.random.standard_normal((HDIM, DIM)) * (1.0 / np.sqrt(HDIM)) / (t * t)[:, None])
    return {"x": x,
            "W1_words": W1_words, "W1_scales": W1_scales,
            "W2_words": W2_words, "W2_scales": W2_scales}


def core(x, W1_words, W1_scales, W2_words, W2_scales):
    pre = mxq(f64(x), 2, "e4m3") @ unpack4(W1_words, W1_scales)
    post = np.square(np.maximum(pre, 0.0))
    out = mxq(post, 2, "e4m3") @ unpack4(W2_words, W2_scales)
    return out


def e4m3fn_bytes(y):
    return np.clip(np.asarray(y, np.float64), -448.0, 448.0).astype(np.float32).astype(ml_dtypes.float8_e4m3fn).view(np.uint8)


def e4m3fn_values(b):
    return np.asarray(b, np.uint8).view(ml_dtypes.float8_e4m3fn).astype(np.float64)


def setup_inputs():
    d = draw0()
    x0 = np.asarray(d['x']).astype(np.float64)
    s = (np.max(np.abs(x0), axis=(0, 1), keepdims=True) / 448.0).astype(np.float32)
    out = {}
    for k, v in d.items():
        if k == 'x':
            out['x_bytes'] = e4m3fn_bytes(x0 / s.astype(np.float64))
            out['x_scale'] = s
        else:
            out[k] = v
    return out


def reference(x_bytes, x_scale, W1_words, W1_scales, W2_words, W2_scales):
    return core(e4m3fn_values(x_bytes) * x_scale.astype(np.float64), W1_words, W1_scales, W2_words, W2_scales)

@@ -1,0 +1,279 @@
+from contextlib import ExitStack
+
+import concourse.mybir as mybir
+from concourse.masks import make_identity
+
+T, K, H, N = 512, 1024, 4096, 1024
+FLOPS = 2 * T * K * H + 2 * T * H * N
+
+F32 = mybir.dt.float32
+BF16 = mybir.dt.bfloat16
+I32 = mybir.dt.int32
+U32 = mybir.dt.uint32
+U8 = mybir.dt.uint8
+FP8 = mybir.dt.float8_e4m3fn
+FP8X4 = mybir.dt.float8_e4m3fn_x4
+FP4X4 = mybir.dt.float4_e2m1fn_x4
+ACT = mybir.ActivationFunctionType
+ALU = mybir.AluOpType
+
+P = 128
+KG = K // 512
+HG = H // 512
+TI = T // P
+NACC = 5
+NPRE = 8 - NACC
+S_TOK = [0,256,256,192,192,192,192,192]
+PERMS = {1: (2, 3), 2: (4,), 3: (5,), 4: (6,), 5: (7,)}
+NB4 = 1
+
+
+def tile_mlp_w4_kernel(tc, x_bytes, x_scale, W1_words, W1_scales, W2_words, W2_scales, out):
+    nc = tc.nc
+    x_in = x_bytes.flatten_outer_dims().rearrange("(i p) k -> p i k", p=P)
+    out_v = out.flatten_outer_dims().rearrange("(i p) n -> i p n", p=P)
+    w1_in = W1_words.rearrange("g p c -> p g c")
+    w2_in = W2_words.rearrange("g p c -> p g c")
+    s1_in = W1_scales.rearrange("g r n -> r g n")
+    s2_in = W2_scales.rearrange("g r n -> r g n")
+
+    with ExitStack() as ctx:
+        keep = ctx.enter_context(tc.tile_pool(name="keep", bufs=1))
+        work = ctx.enter_context(tc.tile_pool(name="work", bufs=3))
+        psum = ctx.enter_context(tc.psum_pool(name="psum", bufs=1))
+        ctx.enter_context(tc.manual_schedule())
+
+        ident = keep.tile([P, P], F32, name="ident")
+        dummy = keep.tile([P, 1], F32, name="dummy")
+        xs = keep.tile([P, KG, 4], F32, name="xs", align_bytes=64)
+        xb = keep.tile([P, TI, K], U8, name="xb", align_bytes=64)
+        s1a = keep.tile([P, KG, 1024], U8, name="s1a", align_bytes=64)
+        s1b = keep.tile([P, KG, H - 1024], U8, name="s1b", align_bytes=64)
+        s2 = keep.tile([P, HG, N], U8, name="s2", align_bytes=64)
+        w2 = keep.tile([P, HG, 2 * N], U8, name="w2", align_bytes=64)
+        xc = keep.tile([P, KG, T], U32, name="xc", align_bytes=64)
+        xsc = keep.tile([P, KG, T], U8, name="xsc", align_bytes=64)
+        w1r0 = keep.tile([P, KG, 1024], U8, name="w1r0", align_bytes=64)
+        w1r1 = keep.tile([P, KG, 1024], U8, name="w1r1", align_bytes=64)
+        w1r = [None] + [keep.tile([P, KG, 2048], U8, name=f"w1raw{c}", align_bytes=64) for c in range(1, HG // 2)]
+        w1p = [keep.tile([P, KG, 4, 256], U8, name=f"w1p{G}", align_bytes=64) for G in range(HG)]
+        s1p = [keep.tile([P, KG, 4, P], U8, name=f"s1p{G}", align_bytes=64) for G in range(HG)]
+        pc = [keep.tile([P, T], U32, name=f"pc{G}", align_bytes=64) for G in range(HG)]
+        psc = [keep.tile([P, T], U8, name=f"psc{G}", align_bytes=64) for G in range(HG)]
+
+        nc.vector.memset(dummy[:], 0.0)
+        nc.vector.memset(s1a[:].rearrange("p g n -> p (g n)").bitcast(I32), 0)
+        nc.vector.memset(s1b[:].rearrange("p g n -> p (g n)").bitcast(I32), 0)
+        make_identity(nc, ident[:])
+        nc.gpsimd.memset(s2[:].rearrange("p g n -> p (g n)").bitcast(I32), 0)
+        nc.scalar.dma_start(out=xs[:], in_=x_scale.rearrange("a b (g p t) -> p (a b g) t", p=P, t=4))
+        nc.scalar.activation(out=dummy[:], in_=dummy[:], func=ACT.Square)
+
+        def load_scales(dst, src):
+            for q in range(4):
+                nc.sync.dma_start(out=dst[32 * q:32 * q + 4].bitcast(I32), in_=src[4 * q:4 * q + 4].bitcast(I32))
+
+        nc.sync.dma_start(out=w1r0[:], in_=w1_in[:, :, 0:1024])
+        nc.sync.dma_start(out=xb[:, 0:2], in_=x_in[:, 0:2])
+        load_scales(s1a, s1_in[:, :, 0:1024])
+        nc.sync.dma_start(out=xb[:, 2:4], in_=x_in[:, 2:4])
+        nc.sync.dma_start(out=w1r1[:], in_=w1_in[:, :, 1024:2048])
+        nc.sync.dma_start(out=w1r[1][:], in_=w1_in[:, :, 2048:4096])
+        load_scales(s1b, s1_in[:, :, 1024:H])
+        for c in range(2, HG // 2):
+            nc.sync.dma_start(out=w1r[c][:], in_=w1_in[:, :, 2048 * c:2048 * (c + 1)])
+        load_scales(s2, s2_in)
+        for c in range(4):
+            nc.sync.dma_start(out=w2[:, 2 * c:2 * c + 2], in_=w2_in[:, 2 * c:2 * c + 2])
+
+        def perm_w(G):
+            for g in range(KG):
+                if G == 0:
+                    raw = w1r0[:, g]
+                elif G == 1:
+                    raw = w1r1[:, g]
+                else:
+                    raw = w1r[G // 2][:, g, 1024 * (G % 2):1024 * (G % 2) + 1024]
+                nc.vector.tensor_copy(
+                    out=w1p[G][:, g].rearrange("p t (m b) -> p t m b", b=2),
+                    in_=raw.rearrange("p (m t b) -> p t m b", t=4, b=2),
+                )
+
+        def perm_s(G):
+            raw = s1a[:, :, 512 * G:512 * (G + 1)] if G < 2 else s1b[:, :, 512 * (G - 2):512 * (G - 1)]
+            nc.vector.tensor_copy(out=s1p[G][:], in_=raw.rearrange("p g (m t) -> p g t m", t=4))
+
+        head_banks = [f"acc{o}" for o in range(NACC)] + ["pre"] * NPRE
+        used = []
+
+        def head_bank(shape):
+            tag = head_banks[len(used) % 8]
+            used.append(tag)
+            return psum.tile(shape, F32, name="hb", tag=tag, bufs=NPRE if tag == "pre" else 1)
+
+        xw = [None] * TI
+        xt = [None] * TI
+        xg = [None] * TI
+
+        def cast(i):
+            xw[i] = work.tile([P, K], BF16, name="xw", align_bytes=64, bufs=4)
+            nc.scalar.copy(out=xw[i][:], in_=xb[:, i].bitcast(FP8))
+
+        def xtr(i):
+            words = xw[i][:].bitcast(F32)
+            xt[i] = head_bank([P, KG, 2, P])
+            for g in range(KG):
+                for u in range(2):
+                    nc.tensor.transpose(xt[i][:, g, u, :], words[:, 256 * g + u:256 * (g + 1):2], ident[:])
+
+        def xtt(i):
+            xg[i] = work.tile([P, KG, P, 4], BF16, name="xg", align_bytes=64)
+            for g in range(KG):
+                nc.vector.tensor_tensor(
+                    out=xg[i][:, g].rearrange("p r (u e) -> p r u e", u=2),
+                    in0=xt[i][:, g].rearrange("p u r -> p (u r)").bitcast(BF16).rearrange("p (u r e) -> p r u e", u=2, e=2),
+                    in1=xs[:, g].rearrange("p (u e) -> p u e", u=2).unsqueeze(1).to_broadcast([P, P, 2, 2]),
+                    op=ALU.mult,
+                )
+
+        def xq(i):
+            for g in range(KG):
+                nc.vector.quantize_mx(
+                    out=xc[:, g, P * i:P * (i + 1)].bitcast(FP8X4),
+                    scales=xsc[:, g, P * i:P * (i + 1)],
+                    in_=xg[i][:, g].rearrange("p r t -> p (r t)"),
+                )
+
+        r = [None] * HG
+        sq = [None] * HG
+
+        def mm1(dst, G, t, g, cols):
+            nc.tensor.matmul_mx(
+                out=dst,
+                lhsT=w1p[G][:, g, t].bitcast(FP4X4),
+                lhsT_scale=s1p[G][:, g, t],
+                rhs=xc[:, g, cols].bitcast(FP8X4),
+                rhs_scale=xsc[:, g, cols],
+                start=(g == 0),
+                stop=(g == KG - 1),
+            )
+
+        def s1h(G, i):
+            if i == 0:
+                r[G] = work.tile([P, T, 4], F32, name="r", align_bytes=64)
+                sq[G] = work.tile([P, T, 4], BF16, name="sq", align_bytes=64)
+            b = head_bank([P, 4, P])
+            cols = slice(P * i, P * (i + 1))
+            for t in range(4):
+                for g in range(KG):
+                    mm1(b[:, t], G, t, g, cols)
+            nc.scalar.activation(out=r[G][:, cols], in_=b[:].rearrange("p t n -> p n t"), func=ACT.Relu)
+
+        def bh(G, i):
+            cols = slice(P * i, P * (i + 1))
+            nc.scalar.activation(out=sq[G][:, cols], in_=r[G][:, cols], func=ACT.Square)
+
+        def s1(G, t):
+            if t == 0:
+                r[G] = work.tile([P, 4, T], F32, name="r", align_bytes=64)
+                sq[G] = work.tile([P, T, 4], BF16, name="sq", align_bytes=64)
+            pre = psum.tile([P, T], F32, name="pre", bufs=NPRE)
+            for g in range(KG):
+                mm1(pre[:], G, t, g, slice(0, T))
+            nc.scalar.activation(out=r[G][:, t], in_=pre[:], func=ACT.Relu)
+
+        def bs(G):
+            n = S_TOK[G]
+            nc.scalar.activation(out=sq[G][:, 0:n], in_=r[G][:, :, 0:n].rearrange("p t n -> p n t"), func=ACT.Square)
+
+        def bv(G):
+            n = S_TOK[G]
+            v = r[G][:, :, n:T].rearrange("p t n -> p n t")
+            nc.vector.tensor_tensor(out=sq[G][:, n:T], in0=v, in1=v, op=ALU.mult)
+
+        def quant(G):
+            nc.vector.quantize_mx(out=pc[G][:].bitcast(FP8X4), scales=psc[G][:], in_=sq[G][:].rearrange("p n t -> p (n t)"))
+
+        outs = [(i, n) for i in range(TI) for n in range(2)]
+        acc = [None] * 8
+
+        def stage2(G, o):
+            i, n = outs[o]
+            if G == 0:
+                if o < NACC:
+                    acc[o] = psum.tile([P, 512], F32, name=f"acc{o}", bufs=1)
+                else:
+                    acc[o] = psum.tile([P, 512], F32, name="pre", bufs=NPRE)
+            nc.tensor.matmul_mx(
+                out=acc[o][:],
+                lhsT=pc[G][:, P * i:P * (i + 1)].bitcast(FP8X4),
+                lhsT_scale=psc[G][:, P * i:P * (i + 1)],
+                rhs=w2[:, G, 1024 * n:1024 * (n + 1)].bitcast(FP4X4),
+                rhs_scale=s2[:, G, 512 * n:512 * (n + 1)],
+                start=(G == 0),
+                stop=(G == HG - 1),
+            )
+
+        def emit(o, parts):
+            i, n = outs[o]
+            res = work.tile([P, 512], F32, name="res", bufs=8)
+            w = 512 // parts
+            for j in range(parts):
+                cols = slice(w * j, w * (j + 1))
+                if (o + j) % 2:
+                    nc.vector.tensor_copy(out=res[:, cols], in_=acc[o][:, cols])
+                else:
+                    nc.scalar.copy(out=res[:, cols], in_=acc[o][:, cols])
+                nc.sync.dma_start(out=out_v[i][:, 512 * n + w * j:512 * n + w * (j + 1)], in_=res[:, cols])
+
+        for i in range(TI):
+            cast(i)
+        perm_w(0)
+        for i in range(TI):
+            xtr(i)
+        xtt(0)
+        perm_s(0)
+        xtt(1)
+        xq(0)
+        s1h(0, 0)
+        xtt(2)
+        xq(1)
+        s1h(0, 1)
+        bh(0, 0)
+        xtt(3)
+        xq(2)
+        s1h(0, 2)
+        bh(0, 1)
+        xq(3)
+        s1h(0, 3)
+        bh(0, 2)
+        perm_s(1)
+        perm_w(1)
+        bh(0, 3)
+
+        for G in range(1, HG):
+            if G >= 2:
+                bv(G - 1)
+            for j in PERMS.get(G, ()):
+                perm_s(j)
+                perm_w(j)
+            for t in range(4):
+                s1(G, t)
+                if t == 0 and G >= 2:
+                    bs(G - 1)
+            if G >= 2:
+                for o in range(NACC):
+                    stage2(G - 2, o)
+            quant(G - 1)
+        bv(HG - 1)
+        bs(HG - 1)
+        quant(HG - 1)
+        for o in range(NACC):
+            stage2(HG - 2, o)
+        for o in range(NACC, NACC + NB4):
+            for G in range(HG - 1):
+                stage2(G, o)
+        for o in range(8):
+            for G in range(HG - 1 if o < NACC + NB4 else 0, HG):
+                stage2(G, o)
+            emit(o, 2 if o == 7 else 1)

@@ -21,11 +21,6 @@ P = 128
 KG = K // 512
 HG = H // 512
 TI = T // P
-NACC = 5
-NPRE = 8 - NACC
-S_TOK = [0,256,256,192,192,192,192,192]
-PERMS = {1: (2, 3), 2: (4,), 3: (5,), 4: (6,), 5: (7,)}
-NB4 = 1
 
 
 def tile_mlp_w4_kernel(tc, x_bytes, x_scale, W1_words, W1_scales, W2_words, W2_scales, out):
@@ -34,7 +29,6 @@ def tile_mlp_w4_kernel(tc, x_bytes, x_scale, W1_words, W1_scales, W2_words, W2_s
     out_v = out.flatten_outer_dims().rearrange("(i p) n -> i p n", p=P)
     w1_in = W1_words.rearrange("g p c -> p g c")
     w2_in = W2_words.rearrange("g p c -> p g c")
-    s1_in = W1_scales.rearrange("g r n -> r g n")
     s2_in = W2_scales.rearrange("g r n -> r g n")
 
     with ExitStack() as ctx:
@@ -47,8 +41,6 @@ def tile_mlp_w4_kernel(tc, x_bytes, x_scale, W1_words, W1_scales, W2_words, W2_s
         dummy = keep.tile([P, 1], F32, name="dummy")
         xs = keep.tile([P, KG, 4], F32, name="xs", align_bytes=64)
         xb = keep.tile([P, TI, K], U8, name="xb", align_bytes=64)
-        s1a = keep.tile([P, KG, 1024], U8, name="s1a", align_bytes=64)
-        s1b = keep.tile([P, KG, H - 1024], U8, name="s1b", align_bytes=64)
         s2 = keep.tile([P, HG, N], U8, name="s2", align_bytes=64)
         w2 = keep.tile([P, HG, 2 * N], U8, name="w2", align_bytes=64)
         xc = keep.tile([P, KG, T], U32, name="xc", align_bytes=64)
@@ -57,15 +49,22 @@ def tile_mlp_w4_kernel(tc, x_bytes, x_scale, W1_words, W1_scales, W2_words, W2_s
         w1r1 = keep.tile([P, KG, 1024], U8, name="w1r1", align_bytes=64)
         w1r = [None] + [keep.tile([P, KG, 2048], U8, name=f"w1raw{c}", align_bytes=64) for c in range(1, HG // 2)]
         w1p = [keep.tile([P, KG, 4, 256], U8, name=f"w1p{G}", align_bytes=64) for G in range(HG)]
-        s1p = [keep.tile([P, KG, 4, P], U8, name=f"s1p{G}", align_bytes=64) for G in range(HG)]
         pc = [keep.tile([P, T], U32, name=f"pc{G}", align_bytes=64) for G in range(HG)]
         psc = [keep.tile([P, T], U8, name=f"psc{G}", align_bytes=64) for G in range(HG)]
+        s1raw = keep.tile([P, 1024], U8, name="s1raw", align_bytes=64)
+        s1t = keep.tile([P, 2, 4, P], U8, name="s1t", align_bytes=64)
+        s1pl = [keep.tile([P, KG, 2, 4, P], U8, name=f"s1pl{h}", align_bytes=64) for h in range(4)]
+
+        def s1p(G, g, t):
+            return s1pl[G // 2][:, g, G % 2, t]
 
         nc.vector.memset(dummy[:], 0.0)
-        nc.vector.memset(s1a[:].rearrange("p g n -> p (g n)").bitcast(I32), 0)
-        nc.vector.memset(s1b[:].rearrange("p g n -> p (g n)").bitcast(I32), 0)
+        zeros = keep.tile([P, 512], BF16, name="zeros")
+        nc.gpsimd.memset(zeros[:].bitcast(I32), 0)
         make_identity(nc, ident[:])
-        nc.gpsimd.memset(s2[:].rearrange("p g n -> p (g n)").bitcast(I32), 0)
+        for h in range(4):
+            (nc.gpsimd if h else nc.vector).memset(s1pl[h][:].rearrange("p g a t m -> p (g a t m)").bitcast(I32), 0)
+        nc.vector.memset(s2[:].rearrange("p g n -> p (g n)").bitcast(I32), 0)
         nc.scalar.dma_start(out=xs[:], in_=x_scale.rearrange("a b (g p t) -> p (a b g) t", p=P, t=4))
         nc.scalar.activation(out=dummy[:], in_=dummy[:], func=ACT.Square)
 
@@ -73,20 +72,45 @@ def tile_mlp_w4_kernel(tc, x_bytes, x_scale, W1_words, W1_scales, W2_words, W2_s
             for q in range(4):
                 nc.sync.dma_start(out=dst[32 * q:32 * q + 4].bitcast(I32), in_=src[4 * q:4 * q + 4].bitcast(I32))
 
-        nc.sync.dma_start(out=w1r0[:], in_=w1_in[:, :, 0:1024])
-        nc.sync.dma_start(out=xb[:, 0:2], in_=x_in[:, 0:2])
-        load_scales(s1a, s1_in[:, :, 0:1024])
-        nc.sync.dma_start(out=xb[:, 2:4], in_=x_in[:, 2:4])
-        nc.sync.dma_start(out=w1r1[:], in_=w1_in[:, :, 1024:2048])
-        nc.sync.dma_start(out=w1r[1][:], in_=w1_in[:, :, 2048:4096])
-        load_scales(s1b, s1_in[:, :, 1024:H])
-        for c in range(2, HG // 2):
+        def move_scales(h):
+            for g in range(KG):
+                for q4 in range(4):
+                    first = 64 * g + 16 * q4 + h
+                    nc.sync.dma_start(
+                        out=s1pl[h][32 * q4:32 * q4 + 4, g].rearrange("p a t m -> p (a t m)").bitcast(I32),
+                        in_=s1t[first:first + 13:4].rearrange("p a t m -> p (a t m)").bitcast(I32),
+                    )
+
+        def load_w1(c):
             nc.sync.dma_start(out=w1r[c][:], in_=w1_in[:, :, 2048 * c:2048 * (c + 1)])
-        load_scales(s2, s2_in)
-        for c in range(4):
+
+        def load_w2(c):
             nc.sync.dma_start(out=w2[:, 2 * c:2 * c + 2], in_=w2_in[:, 2 * c:2 * c + 2])
 
-        def perm_w(G):
+        nc.sync.dma_start(out=s1raw[:].bitcast(I32), in_=W1_scales.rearrange("g r (h n) -> (g r h) n", h=4).bitcast(I32))
+        nc.sync.dma_start(out=xb[:, 0:1], in_=x_in[:, 0:1])
+        nc.sync.dma_start(out=w1r0[:], in_=w1_in[:, :, 0:1024])
+        nc.sync.dma_start(out=xb[:, 1:2], in_=x_in[:, 1:2])
+        nc.sync.dma_start(out=xb[:, 2:4], in_=x_in[:, 2:4])
+        nc.vector.tensor_copy(
+            out=s1t[:],
+            in_=s1raw[:].rearrange("p (a m t) -> p a t m", a=2, t=4),
+        )
+        move_scales(0)
+        nc.sync.dma_start(out=w1r1[:], in_=w1_in[:, :, 1024:2048])
+        load_w1(1)
+        move_scales(1)
+        load_w1(2)
+        load_scales(s2, s2_in)
+        load_w2(0)
+        move_scales(2)
+        load_w1(3)
+        load_w2(1)
+        move_scales(3)
+        load_w2(2)
+        load_w2(3)
+
+        def pw(G):
             for g in range(KG):
                 if G == 0:
                     raw = w1r0[:, g]
@@ -99,17 +123,17 @@ def tile_mlp_w4_kernel(tc, x_bytes, x_scale, W1_words, W1_scales, W2_words, W2_s
                     in_=raw.rearrange("p (m t b) -> p t m b", t=4, b=2),
                 )
 
-        def perm_s(G):
-            raw = s1a[:, :, 512 * G:512 * (G + 1)] if G < 2 else s1b[:, :, 512 * (G - 2):512 * (G - 1)]
-            nc.vector.tensor_copy(out=s1p[G][:], in_=raw.rearrange("p g (m t) -> p g t m", t=4))
 
-        head_banks = [f"acc{o}" for o in range(NACC)] + ["pre"] * NPRE
-        used = []
+        bank = [None] * 8
 
-        def head_bank(shape):
-            tag = head_banks[len(used) % 8]
-            used.append(tag)
-            return psum.tile(shape, F32, name="hb", tag=tag, bufs=NPRE if tag == "pre" else 1)
+        def new_bank(shape, b):
+            return psum.tile(shape, F32, name=f"bank{b}", bufs=1)
+
+        scratch = new_bank([P, 512], 7)
+
+        def warm(n):
+            for _ in range(n):
+                nc.tensor.matmul(scratch[:], lhsT=zeros[:, 0:P], rhs=zeros[:], start=True, stop=True)
 
         xw = [None] * TI
         xt = [None] * TI
@@ -119,19 +143,40 @@ def tile_mlp_w4_kernel(tc, x_bytes, x_scale, W1_words, W1_scales, W2_words, W2_s
             xw[i] = work.tile([P, K], BF16, name="xw", align_bytes=64, bufs=4)
             nc.scalar.copy(out=xw[i][:], in_=xb[:, i].bitcast(FP8))
 
-        def xtr(i):
+        def cast0():
+            xw[0] = work.tile([P, K], BF16, name="xw", align_bytes=64, bufs=4)
+            for g in range(KG):
+                nc.scalar.copy(out=xw[0][:, 512 * g:512 * (g + 1)], in_=xb[:, 0, 512 * g:512 * (g + 1)].bitcast(FP8))
+
+        def xtr0():
+            words = xw[0][:].bitcast(F32)
+            xt[0] = []
+            for g in range(KG):
+                b = new_bank([P, 2, P], 6 * g)
+                xt[0].append(b)
+                for u in range(2):
+                    nc.tensor.transpose(b[:, u, :], words[:, 256 * g + u:256 * (g + 1):2], ident[:])
+
+        def castv(i):
+            xw[i] = work.tile([P, K], BF16, name="xw", align_bytes=64, bufs=4)
+            nc.vector.tensor_copy(out=xw[i][:], in_=xb[:, i].bitcast(FP8))
+
+        def xtr(i, b):
             words = xw[i][:].bitcast(F32)
-            xt[i] = head_bank([P, KG, 2, P])
+            xt[i] = new_bank([P, KG, 2, P], b)
             for g in range(KG):
                 for u in range(2):
                     nc.tensor.transpose(xt[i][:, g, u, :], words[:, 256 * g + u:256 * (g + 1):2], ident[:])
 
-        def xtt(i):
+        def xtt0():
+            xtt(0, True)
+
+        def xtt(i, split=False):
             xg[i] = work.tile([P, KG, P, 4], BF16, name="xg", align_bytes=64)
             for g in range(KG):
                 nc.vector.tensor_tensor(
                     out=xg[i][:, g].rearrange("p r (u e) -> p r u e", u=2),
-                    in0=xt[i][:, g].rearrange("p u r -> p (u r)").bitcast(BF16).rearrange("p (u r e) -> p r u e", u=2, e=2),
+                    in0=(xt[i][g][:] if split else xt[i][:, g]).rearrange("p u r -> p (u r)").bitcast(BF16).rearrange("p (u r e) -> p r u e", u=2, e=2),
                     in1=xs[:, g].rearrange("p (u e) -> p u e", u=2).unsqueeze(1).to_broadcast([P, P, 2, 2]),
                     op=ALU.mult,
                 )
@@ -146,64 +191,75 @@ def tile_mlp_w4_kernel(tc, x_bytes, x_scale, W1_words, W1_scales, W2_words, W2_s
 
         r = [None] * HG
         sq = [None] * HG
+        pre = {}
 
         def mm1(dst, G, t, g, cols):
             nc.tensor.matmul_mx(
                 out=dst,
                 lhsT=w1p[G][:, g, t].bitcast(FP4X4),
-                lhsT_scale=s1p[G][:, g, t],
+                lhsT_scale=s1p(G, g, t),
                 rhs=xc[:, g, cols].bitcast(FP8X4),
                 rhs_scale=xsc[:, g, cols],
                 start=(g == 0),
                 stop=(g == KG - 1),
             )
 
-        def s1h(G, i):
+        def h1(G, i, b):
             if i == 0:
                 r[G] = work.tile([P, T, 4], F32, name="r", align_bytes=64)
                 sq[G] = work.tile([P, T, 4], BF16, name="sq", align_bytes=64)
-            b = head_bank([P, 4, P])
+            pre[G, i] = new_bank([P, 4, P], b)
             cols = slice(P * i, P * (i + 1))
             for t in range(4):
                 for g in range(KG):
-                    mm1(b[:, t], G, t, g, cols)
-            nc.scalar.activation(out=r[G][:, cols], in_=b[:].rearrange("p t n -> p n t"), func=ACT.Relu)
+                    mm1(pre[G, i][:, t], G, t, g, cols)
 
-        def bh(G, i):
+        def hA(G, i):
+            nc.scalar.activation(out=r[G][:, P * i:P * (i + 1)], in_=pre[G, i][:].rearrange("p t n -> p n t"), func=ACT.Relu)
+
+        def hB(G, i):
             cols = slice(P * i, P * (i + 1))
             nc.scalar.activation(out=sq[G][:, cols], in_=r[G][:, cols], func=ACT.Square)
 
-        def s1(G, t):
+        def hBv(G, i):
+            cols = slice(P * i, P * (i + 1))
+            nc.vector.tensor_tensor(out=sq[G][:, cols], in0=r[G][:, cols], in1=r[G][:, cols], op=ALU.mult)
+
+        def n1(G, t, b):
             if t == 0:
                 r[G] = work.tile([P, 4, T], F32, name="r", align_bytes=64)
                 sq[G] = work.tile([P, T, 4], BF16, name="sq", align_bytes=64)
-            pre = psum.tile([P, T], F32, name="pre", bufs=NPRE)
+            pre[G, t] = new_bank([P, T], b)
             for g in range(KG):
-                mm1(pre[:], G, t, g, slice(0, T))
-            nc.scalar.activation(out=r[G][:, t], in_=pre[:], func=ACT.Relu)
+                mm1(pre[G, t][:], G, t, g, slice(0, T))
 
-        def bs(G):
-            n = S_TOK[G]
-            nc.scalar.activation(out=sq[G][:, 0:n], in_=r[G][:, :, 0:n].rearrange("p t n -> p n t"), func=ACT.Square)
+        def nA(G, t):
+            nc.scalar.activation(out=r[G][:, t], in_=pre[G, t][:], func=ACT.Relu)
 
-        def bv(G):
-            n = S_TOK[G]
-            v = r[G][:, :, n:T].rearrange("p t n -> p n t")
-            nc.vector.tensor_tensor(out=sq[G][:, n:T], in0=v, in1=v, op=ALU.mult)
+        def tok4(ap):
+            return ap.rearrange("p (c i) t -> p c t i", i=4)
 
-        def quant(G):
+        def bs(G, n0, n1_):
+            nc.scalar.activation(
+                out=tok4(sq[G][:, n0:n1_]),
+                in_=r[G][:, :, n0:n1_].rearrange("p t (c i) -> p c t i", i=4),
+                func=ACT.Square,
+            )
+
+        def bv(G, n0, n1_):
+            v = r[G][:, :, n0:n1_].rearrange("p t (c i) -> p c t i", i=4)
+            nc.vector.tensor_tensor(out=tok4(sq[G][:, n0:n1_]), in0=v, in1=v, op=ALU.mult)
+
+        def q(G):
             nc.vector.quantize_mx(out=pc[G][:].bitcast(FP8X4), scales=psc[G][:], in_=sq[G][:].rearrange("p n t -> p (n t)"))
 
         outs = [(i, n) for i in range(TI) for n in range(2)]
         acc = [None] * 8
 
-        def stage2(G, o):
+        def s2m(G, o, b=None):
             i, n = outs[o]
             if G == 0:
-                if o < NACC:
-                    acc[o] = psum.tile([P, 512], F32, name=f"acc{o}", bufs=1)
-                else:
-                    acc[o] = psum.tile([P, 512], F32, name="pre", bufs=NPRE)
+                acc[o] = new_bank([P, 512], b)
             nc.tensor.matmul_mx(
                 out=acc[o][:],
                 lhsT=pc[G][:, P * i:P * (i + 1)].bitcast(FP8X4),
@@ -214,66 +270,208 @@ def tile_mlp_w4_kernel(tc, x_bytes, x_scale, W1_words, W1_scales, W2_words, W2_s
                 stop=(G == HG - 1),
             )
 
-        def emit(o, parts):
+        res = [None] * 8
+
+        def ev(o, engine, j, parts):
             i, n = outs[o]
-            res = work.tile([P, 512], F32, name="res", bufs=8)
+            if j == 0:
+                res[o] = work.tile([P, 512], F32, name="res", bufs=8)
             w = 512 // parts
-            for j in range(parts):
-                cols = slice(w * j, w * (j + 1))
-                if (o + j) % 2:
-                    nc.vector.tensor_copy(out=res[:, cols], in_=acc[o][:, cols])
-                else:
-                    nc.scalar.copy(out=res[:, cols], in_=acc[o][:, cols])
-                nc.sync.dma_start(out=out_v[i][:, 512 * n + w * j:512 * n + w * (j + 1)], in_=res[:, cols])
+            cols = slice(w * j, w * (j + 1))
+            if engine == "V":
+                nc.vector.tensor_copy(out=res[o][:, cols], in_=acc[o][:, cols])
+            else:
+                nc.scalar.copy(out=res[o][:, cols], in_=acc[o][:, cols])
+            (nc.scalar if parts == 2 and engine == "S" else nc.sync).dma_start(out=out_v[i][:, 512 * n + w * j:512 * n + w * (j + 1)], in_=res[o][:, cols])
 
-        for i in range(TI):
-            cast(i)
-        perm_w(0)
-        for i in range(TI):
-            xtr(i)
-        xtt(0)
-        perm_s(0)
-        xtt(1)
+        cast0()
+        cast(1)
+        cast(2)
+        cast(3)
+        pw(0)
+        warm(5)
+        xtr0()
+        warm(1)
+        xtt0()
         xq(0)
-        s1h(0, 0)
-        xtt(2)
+        xtr(1, 1)
+        warm(2)
+        xtr(2, 2)
+        warm(1)
+        h1(0, 0, 3)
+        hA(0, 0)
+        xtt(1)
         xq(1)
-        s1h(0, 1)
-        bh(0, 0)
-        xtt(3)
+        xtr(3, 4)
+        h1(0, 1, 5)
+        hB(0, 0)
+        hA(0, 1)
+        xtt(2)
         xq(2)
-        s1h(0, 2)
-        bh(0, 1)
+        h1(0, 2, 6)
+        hB(0, 1)
+        hA(0, 2)
+        xtt(3)
         xq(3)
-        s1h(0, 3)
-        bh(0, 2)
-        perm_s(1)
-        perm_w(1)
-        bh(0, 3)
-
-        for G in range(1, HG):
-            if G >= 2:
-                bv(G - 1)
-            for j in PERMS.get(G, ()):
-                perm_s(j)
-                perm_w(j)
-            for t in range(4):
-                s1(G, t)
-                if t == 0 and G >= 2:
-                    bs(G - 1)
-            if G >= 2:
-                for o in range(NACC):
-                    stage2(G - 2, o)
-            quant(G - 1)
-        bv(HG - 1)
-        bs(HG - 1)
-        quant(HG - 1)
-        for o in range(NACC):
-            stage2(HG - 2, o)
-        for o in range(NACC, NACC + NB4):
-            for G in range(HG - 1):
-                stage2(G, o)
-        for o in range(8):
-            for G in range(HG - 1 if o < NACC + NB4 else 0, HG):
-                stage2(G, o)
-            emit(o, 2 if o == 7 else 1)
+        h1(0, 3, 7)
+        hB(0, 2)
+        hA(0, 3)
+        pw(1)
+        hB(0, 3)
+        pw(2)
+        pw(3)
+        pw(4)
+        n1(1, 0, 0)
+        nA(1, 0)
+        n1(1, 1, 1)
+        nA(1, 1)
+        n1(1, 2, 2)
+        nA(1, 2)
+        n1(1, 3, 3)
+        nA(1, 3)
+        q(0)
+        bv(1, 128, 512)
+        n1(2, 0, 4)
+        nA(2, 0)
+        bs(1, 0, 128)
+        n1(2, 1, 5)
+        nA(2, 1)
+        n1(2, 2, 6)
+        nA(2, 2)
+        n1(2, 3, 7)
+        nA(2, 3)
+        s2m(0, 0, 0)
+        s2m(0, 1, 1)
+        s2m(0, 2, 2)
+        s2m(0, 3, 3)
+        s2m(0, 4, 4)
+        q(1)
+        bv(2, 224, 512)
+        pw(6)
+        n1(3, 0, 5)
+        nA(3, 0)
+        bs(2, 0, 224)
+        n1(3, 1, 6)
+        nA(3, 1)
+        n1(3, 2, 7)
+        nA(3, 2)
+        n1(3, 3, 5)
+        nA(3, 3)
+        s2m(1, 0)
+        s2m(1, 1)
+        s2m(1, 2)
+        s2m(1, 3)
+        s2m(1, 4)
+        q(2)
+        pw(5)
+        bv(3, 224, 512)
+        n1(4, 0, 6)
+        nA(4, 0)
+        bs(3, 0, 224)
+        n1(4, 1, 7)
+        nA(4, 1)
+        n1(4, 2, 5)
+        nA(4, 2)
+        n1(4, 3, 6)
+        nA(4, 3)
+        s2m(2, 0)
+        s2m(2, 1)
+        s2m(2, 2)
+        s2m(2, 3)
+        s2m(2, 4)
+        q(3)
+        bv(4, 224, 512)
+        pw(7)
+        n1(5, 0, 7)
+        nA(5, 0)
+        bs(4, 0, 224)
+        n1(5, 1, 5)
+        nA(5, 1)
+        n1(5, 2, 6)
+        nA(5, 2)
+        n1(5, 3, 7)
+        nA(5, 3)
+        s2m(3, 0)
+        s2m(3, 1)
+        s2m(3, 2)
+        s2m(3, 3)
+        s2m(3, 4)
+        q(4)
+        bv(5, 96, 512)
+        n1(6, 0, 5)
+        nA(6, 0)
+        bs(5, 0, 96)
+        n1(6, 1, 6)
+        nA(6, 1)
+        n1(6, 2, 7)
+        nA(6, 2)
+        n1(6, 3, 5)
+        nA(6, 3)
+        s2m(4, 0)
+        s2m(4, 1)
+        s2m(4, 2)
+        s2m(4, 3)
+        s2m(4, 4)
+        q(5)
+        bv(6, 160, 512)
+        n1(7, 0, 6)
+        nA(7, 0)
+        bs(6, 0, 160)
+        n1(7, 1, 7)
+        nA(7, 1)
+        n1(7, 2, 5)
+        nA(7, 2)
+        n1(7, 3, 6)
+        nA(7, 3)
+        s2m(5, 0)
+        s2m(5, 1)
+        s2m(5, 2)
+        s2m(5, 3)
+        s2m(5, 4)
+        q(6)
+        bv(7, 256, 512)
+        bs(7, 0, 256)
+        q(7)
+        s2m(6, 0)
+        s2m(6, 1)
+        s2m(6, 2)
+        s2m(6, 3)
+        s2m(6, 4)
+        s2m(0, 5, 7)
+        s2m(1, 5)
+        s2m(2, 5)
+        s2m(3, 5)
+        s2m(4, 5)
+        s2m(5, 5)
+        s2m(6, 5)
+        s2m(7, 0)
+        ev(0, "S", 0, 1)
+        s2m(7, 1)
+        ev(1, "V", 0, 1)
+        s2m(7, 2)
+        ev(2, "S", 0, 1)
+        s2m(7, 3)
+        ev(3, "V", 0, 1)
+        s2m(7, 4)
+        ev(4, "S", 0, 1)
+        s2m(7, 5)
+        ev(5, "V", 0, 1)
+        s2m(0, 6, 5)
+        s2m(1, 6)
+        s2m(2, 6)
+        s2m(3, 6)
+        s2m(4, 6)
+        s2m(5, 6)
+        s2m(6, 6)
+        s2m(7, 6)
+        ev(6, "S", 0, 1)
+        s2m(0, 7, 6)
+        s2m(1, 7)
+        s2m(2, 7)
+        s2m(3, 7)
+        s2m(4, 7)
+        s2m(5, 7)
+        s2m(6, 7)
+        s2m(7, 7)
+        ev(7, "V", 0, 2)
+        ev(7, "S", 1, 2)

from contextlib import ExitStack

import concourse.mybir as mybir
from concourse.masks import make_identity

T, K, H, N = 512, 1024, 4096, 1024
FLOPS = 2 * T * K * H + 2 * T * H * N

F32 = mybir.dt.float32
BF16 = mybir.dt.bfloat16
I32 = mybir.dt.int32
U32 = mybir.dt.uint32
U8 = mybir.dt.uint8
FP8 = mybir.dt.float8_e4m3fn
FP8X4 = mybir.dt.float8_e4m3fn_x4
FP4X4 = mybir.dt.float4_e2m1fn_x4
ACT = mybir.ActivationFunctionType
ALU = mybir.AluOpType

P = 128
KG = K // 512
HG = H // 512
TI = T // P


def tile_mlp_w4_kernel(tc, x_bytes, x_scale, W1_words, W1_scales, W2_words, W2_scales, out):
    nc = tc.nc
    x_in = x_bytes.flatten_outer_dims().rearrange("(i p) k -> p i k", p=P)
    out_v = out.flatten_outer_dims().rearrange("(i p) n -> i p n", p=P)
    w1_in = W1_words.rearrange("g p c -> p g c")
    w2_in = W2_words.rearrange("g p c -> p g c")
    s2_in = W2_scales.rearrange("g r n -> r g n")

    with ExitStack() as ctx:
        keep = ctx.enter_context(tc.tile_pool(name="keep", bufs=1))
        work = ctx.enter_context(tc.tile_pool(name="work", bufs=3))
        psum = ctx.enter_context(tc.psum_pool(name="psum", bufs=1))
        ctx.enter_context(tc.manual_schedule())

        ident = keep.tile([P, P], F32, name="ident")
        dummy = keep.tile([P, 1], F32, name="dummy")
        xs = keep.tile([P, KG, 4], F32, name="xs", align_bytes=64)
        xb = keep.tile([P, TI, K], U8, name="xb", align_bytes=64)
        s2 = keep.tile([P, HG, N], U8, name="s2", align_bytes=64)
        w2 = keep.tile([P, HG, 2 * N], U8, name="w2", align_bytes=64)
        xc = keep.tile([P, KG, T], U32, name="xc", align_bytes=64)
        xsc = keep.tile([P, KG, T], U8, name="xsc", align_bytes=64)
        w1r0 = keep.tile([P, KG, 1024], U8, name="w1r0", align_bytes=64)
        w1r1 = keep.tile([P, KG, 1024], U8, name="w1r1", align_bytes=64)
        w1r = [None] + [keep.tile([P, KG, 2048], U8, name=f"w1raw{c}", align_bytes=64) for c in range(1, HG // 2)]
        w1p = [keep.tile([P, KG, 4, 256], U8, name=f"w1p{G}", align_bytes=64) for G in range(HG)]
        pc = [keep.tile([P, T], U32, name=f"pc{G}", align_bytes=64) for G in range(HG)]
        psc = [keep.tile([P, T], U8, name=f"psc{G}", align_bytes=64) for G in range(HG)]
        s1raw = keep.tile([P, 1024], U8, name="s1raw", align_bytes=64)
        s1t = keep.tile([P, 2, 4, P], U8, name="s1t", align_bytes=64)
        s1pl = [keep.tile([P, KG, 2, 4, P], U8, name=f"s1pl{h}", align_bytes=64) for h in range(4)]

        def s1p(G, g, t):
            return s1pl[G // 2][:, g, G % 2, t]

        nc.vector.memset(dummy[:], 0.0)
        zeros = keep.tile([P, 512], BF16, name="zeros")
        nc.gpsimd.memset(zeros[:].bitcast(I32), 0)
        make_identity(nc, ident[:])
        for h in range(4):
            (nc.gpsimd if h else nc.vector).memset(s1pl[h][:].rearrange("p g a t m -> p (g a t m)").bitcast(I32), 0)
        nc.vector.memset(s2[:].rearrange("p g n -> p (g n)").bitcast(I32), 0)
        nc.scalar.dma_start(out=xs[:], in_=x_scale.rearrange("a b (g p t) -> p (a b g) t", p=P, t=4))
        nc.scalar.activation(out=dummy[:], in_=dummy[:], func=ACT.Square)

        def load_scales(dst, src):
            for q in range(4):
                nc.sync.dma_start(out=dst[32 * q:32 * q + 4].bitcast(I32), in_=src[4 * q:4 * q + 4].bitcast(I32))

        def move_scales(h):
            for g in range(KG):
                for q4 in range(4):
                    first = 64 * g + 16 * q4 + h
                    nc.sync.dma_start(
                        out=s1pl[h][32 * q4:32 * q4 + 4, g].rearrange("p a t m -> p (a t m)").bitcast(I32),
                        in_=s1t[first:first + 13:4].rearrange("p a t m -> p (a t m)").bitcast(I32),
                    )

        def load_w1(c):
            nc.sync.dma_start(out=w1r[c][:], in_=w1_in[:, :, 2048 * c:2048 * (c + 1)])

        def load_w2(c):
            nc.sync.dma_start(out=w2[:, 2 * c:2 * c + 2], in_=w2_in[:, 2 * c:2 * c + 2])

        nc.sync.dma_start(out=s1raw[:].bitcast(I32), in_=W1_scales.rearrange("g r (h n) -> (g r h) n", h=4).bitcast(I32))
        nc.sync.dma_start(out=xb[:, 0:1], in_=x_in[:, 0:1])
        nc.sync.dma_start(out=w1r0[:], in_=w1_in[:, :, 0:1024])
        nc.sync.dma_start(out=xb[:, 1:2], in_=x_in[:, 1:2])
        nc.sync.dma_start(out=xb[:, 2:4], in_=x_in[:, 2:4])
        nc.vector.tensor_copy(
            out=s1t[:],
            in_=s1raw[:].rearrange("p (a m t) -> p a t m", a=2, t=4),
        )
        move_scales(0)
        nc.sync.dma_start(out=w1r1[:], in_=w1_in[:, :, 1024:2048])
        load_w1(1)
        move_scales(1)
        load_w1(2)
        load_scales(s2, s2_in)
        load_w2(0)
        move_scales(2)
        load_w1(3)
        load_w2(1)
        move_scales(3)
        load_w2(2)
        load_w2(3)

        def pw(G):
            for g in range(KG):
                if G == 0:
                    raw = w1r0[:, g]
                elif G == 1:
                    raw = w1r1[:, g]
                else:
                    raw = w1r[G // 2][:, g, 1024 * (G % 2):1024 * (G % 2) + 1024]
                nc.vector.tensor_copy(
                    out=w1p[G][:, g].rearrange("p t (m b) -> p t m b", b=2),
                    in_=raw.rearrange("p (m t b) -> p t m b", t=4, b=2),
                )


        bank = [None] * 8

        def new_bank(shape, b):
            return psum.tile(shape, F32, name=f"bank{b}", bufs=1)

        scratch = new_bank([P, 512], 7)

        def warm(n):
            for _ in range(n):
                nc.tensor.matmul(scratch[:], lhsT=zeros[:, 0:P], rhs=zeros[:], start=True, stop=True)

        xw = [None] * TI
        xt = [None] * TI
        xg = [None] * TI

        def cast(i):
            xw[i] = work.tile([P, K], BF16, name="xw", align_bytes=64, bufs=4)
            nc.scalar.copy(out=xw[i][:], in_=xb[:, i].bitcast(FP8))

        def cast0():
            xw[0] = work.tile([P, K], BF16, name="xw", align_bytes=64, bufs=4)
            for g in range(KG):
                nc.scalar.copy(out=xw[0][:, 512 * g:512 * (g + 1)], in_=xb[:, 0, 512 * g:512 * (g + 1)].bitcast(FP8))

        def xtr0():
            words = xw[0][:].bitcast(F32)
            xt[0] = []
            for g in range(KG):
                b = new_bank([P, 2, P], 6 * g)
                xt[0].append(b)
                for u in range(2):
                    nc.tensor.transpose(b[:, u, :], words[:, 256 * g + u:256 * (g + 1):2], ident[:])

        def castv(i):
            xw[i] = work.tile([P, K], BF16, name="xw", align_bytes=64, bufs=4)
            nc.vector.tensor_copy(out=xw[i][:], in_=xb[:, i].bitcast(FP8))

        def xtr(i, b):
            words = xw[i][:].bitcast(F32)
            xt[i] = new_bank([P, KG, 2, P], b)
            for g in range(KG):
                for u in range(2):
                    nc.tensor.transpose(xt[i][:, g, u, :], words[:, 256 * g + u:256 * (g + 1):2], ident[:])

        def xtt0():
            xtt(0, True)

        def xtt(i, split=False):
            xg[i] = work.tile([P, KG, P, 4], BF16, name="xg", align_bytes=64)
            for g in range(KG):
                nc.vector.tensor_tensor(
                    out=xg[i][:, g].rearrange("p r (u e) -> p r u e", u=2),
                    in0=(xt[i][g][:] if split else xt[i][:, g]).rearrange("p u r -> p (u r)").bitcast(BF16).rearrange("p (u r e) -> p r u e", u=2, e=2),
                    in1=xs[:, g].rearrange("p (u e) -> p u e", u=2).unsqueeze(1).to_broadcast([P, P, 2, 2]),
                    op=ALU.mult,
                )

        def xq(i):
            for g in range(KG):
                nc.vector.quantize_mx(
                    out=xc[:, g, P * i:P * (i + 1)].bitcast(FP8X4),
                    scales=xsc[:, g, P * i:P * (i + 1)],
                    in_=xg[i][:, g].rearrange("p r t -> p (r t)"),
                )

        r = [None] * HG
        sq = [None] * HG
        pre = {}

        def mm1(dst, G, t, g, cols):
            nc.tensor.matmul_mx(
                out=dst,
                lhsT=w1p[G][:, g, t].bitcast(FP4X4),
                lhsT_scale=s1p(G, g, t),
                rhs=xc[:, g, cols].bitcast(FP8X4),
                rhs_scale=xsc[:, g, cols],
                start=(g == 0),
                stop=(g == KG - 1),
            )

        def h1(G, i, b):
            if i == 0:
                r[G] = work.tile([P, T, 4], F32, name="r", align_bytes=64)
                sq[G] = work.tile([P, T, 4], BF16, name="sq", align_bytes=64)
            pre[G, i] = new_bank([P, 4, P], b)
            cols = slice(P * i, P * (i + 1))
            for t in range(4):
                for g in range(KG):
                    mm1(pre[G, i][:, t], G, t, g, cols)

        def hA(G, i):
            nc.scalar.activation(out=r[G][:, P * i:P * (i + 1)], in_=pre[G, i][:].rearrange("p t n -> p n t"), func=ACT.Relu)

        def hB(G, i):
            cols = slice(P * i, P * (i + 1))
            nc.scalar.activation(out=sq[G][:, cols], in_=r[G][:, cols], func=ACT.Square)

        def hBv(G, i):
            cols = slice(P * i, P * (i + 1))
            nc.vector.tensor_tensor(out=sq[G][:, cols], in0=r[G][:, cols], in1=r[G][:, cols], op=ALU.mult)

        def n1(G, t, b):
            if t == 0:
                r[G] = work.tile([P, 4, T], F32, name="r", align_bytes=64)
                sq[G] = work.tile([P, T, 4], BF16, name="sq", align_bytes=64)
            pre[G, t] = new_bank([P, T], b)
            for g in range(KG):
                mm1(pre[G, t][:], G, t, g, slice(0, T))

        def nA(G, t):
            nc.scalar.activation(out=r[G][:, t], in_=pre[G, t][:], func=ACT.Relu)

        def tok4(ap):
            return ap.rearrange("p (c i) t -> p c t i", i=4)

        def bs(G, n0, n1_):
            nc.scalar.activation(
                out=tok4(sq[G][:, n0:n1_]),
                in_=r[G][:, :, n0:n1_].rearrange("p t (c i) -> p c t i", i=4),
                func=ACT.Square,
            )

        def bv(G, n0, n1_):
            v = r[G][:, :, n0:n1_].rearrange("p t (c i) -> p c t i", i=4)
            nc.vector.tensor_tensor(out=tok4(sq[G][:, n0:n1_]), in0=v, in1=v, op=ALU.mult)

        def q(G):
            nc.vector.quantize_mx(out=pc[G][:].bitcast(FP8X4), scales=psc[G][:], in_=sq[G][:].rearrange("p n t -> p (n t)"))

        outs = [(i, n) for i in range(TI) for n in range(2)]
        acc = [None] * 8

        def s2m(G, o, b=None):
            i, n = outs[o]
            if G == 0:
                acc[o] = new_bank([P, 512], b)
            nc.tensor.matmul_mx(
                out=acc[o][:],
                lhsT=pc[G][:, P * i:P * (i + 1)].bitcast(FP8X4),
                lhsT_scale=psc[G][:, P * i:P * (i + 1)],
                rhs=w2[:, G, 1024 * n:1024 * (n + 1)].bitcast(FP4X4),
                rhs_scale=s2[:, G, 512 * n:512 * (n + 1)],
                start=(G == 0),
                stop=(G == HG - 1),
            )

        res = [None] * 8

        def ev(o, engine, j, parts):
            i, n = outs[o]
            if j == 0:
                res[o] = work.tile([P, 512], F32, name="res", bufs=8)
            w = 512 // parts
            cols = slice(w * j, w * (j + 1))
            if engine == "V":
                nc.vector.tensor_copy(out=res[o][:, cols], in_=acc[o][:, cols])
            else:
                nc.scalar.copy(out=res[o][:, cols], in_=acc[o][:, cols])
            (nc.scalar if parts == 2 and engine == "S" else nc.sync).dma_start(out=out_v[i][:, 512 * n + w * j:512 * n + w * (j + 1)], in_=res[o][:, cols])

        cast0()
        cast(1)
        cast(2)
        cast(3)
        pw(0)
        warm(5)
        xtr0()
        warm(1)
        xtt0()
        xq(0)
        xtr(1, 1)
        warm(2)
        xtr(2, 2)
        warm(1)
        h1(0, 0, 3)
        hA(0, 0)
        xtt(1)
        xq(1)
        xtr(3, 4)
        h1(0, 1, 5)
        hB(0, 0)
        hA(0, 1)
        xtt(2)
        xq(2)
        h1(0, 2, 6)
        hB(0, 1)
        hA(0, 2)
        xtt(3)
        xq(3)
        h1(0, 3, 7)
        hB(0, 2)
        hA(0, 3)
        pw(1)
        hB(0, 3)
        pw(2)
        pw(3)
        pw(4)
        n1(1, 0, 0)
        nA(1, 0)
        n1(1, 1, 1)
        nA(1, 1)
        n1(1, 2, 2)
        nA(1, 2)
        n1(1, 3, 3)
        nA(1, 3)
        q(0)
        bv(1, 128, 512)
        n1(2, 0, 4)
        nA(2, 0)
        bs(1, 0, 128)
        n1(2, 1, 5)
        nA(2, 1)
        n1(2, 2, 6)
        nA(2, 2)
        n1(2, 3, 7)
        nA(2, 3)
        s2m(0, 0, 0)
        s2m(0, 1, 1)
        s2m(0, 2, 2)
        s2m(0, 3, 3)
        s2m(0, 4, 4)
        q(1)
        bv(2, 224, 512)
        pw(6)
        n1(3, 0, 5)
        nA(3, 0)
        bs(2, 0, 224)
        n1(3, 1, 6)
        nA(3, 1)
        n1(3, 2, 7)
        nA(3, 2)
        n1(3, 3, 5)
        nA(3, 3)
        s2m(1, 0)
        s2m(1, 1)
        s2m(1, 2)
        s2m(1, 3)
        s2m(1, 4)
        q(2)
        pw(5)
        bv(3, 224, 512)
        n1(4, 0, 6)
        nA(4, 0)
        bs(3, 0, 224)
        n1(4, 1, 7)
        nA(4, 1)
        n1(4, 2, 5)
        nA(4, 2)
        n1(4, 3, 6)
        nA(4, 3)
        s2m(2, 0)
        s2m(2, 1)
        s2m(2, 2)
        s2m(2, 3)
        s2m(2, 4)
        q(3)
        bv(4, 224, 512)
        pw(7)
        n1(5, 0, 7)
        nA(5, 0)
        bs(4, 0, 224)
        n1(5, 1, 5)
        nA(5, 1)
        n1(5, 2, 6)
        nA(5, 2)
        n1(5, 3, 7)
        nA(5, 3)
        s2m(3, 0)
        s2m(3, 1)
        s2m(3, 2)
        s2m(3, 3)
        s2m(3, 4)
        q(4)
        bv(5, 96, 512)
        n1(6, 0, 5)
        nA(6, 0)
        bs(5, 0, 96)
        n1(6, 1, 6)
        nA(6, 1)
        n1(6, 2, 7)
        nA(6, 2)
        n1(6, 3, 5)
        nA(6, 3)
        s2m(4, 0)
        s2m(4, 1)
        s2m(4, 2)
        s2m(4, 3)
        s2m(4, 4)
        q(5)
        bv(6, 160, 512)
        n1(7, 0, 6)
        nA(7, 0)
        bs(6, 0, 160)
        n1(7, 1, 7)
        nA(7, 1)
        n1(7, 2, 5)
        nA(7, 2)
        n1(7, 3, 6)
        nA(7, 3)
        s2m(5, 0)
        s2m(5, 1)
        s2m(5, 2)
        s2m(5, 3)
        s2m(5, 4)
        q(6)
        bv(7, 256, 512)
        bs(7, 0, 256)
        q(7)
        s2m(6, 0)
        s2m(6, 1)
        s2m(6, 2)
        s2m(6, 3)
        s2m(6, 4)
        s2m(0, 5, 7)
        s2m(1, 5)
        s2m(2, 5)
        s2m(3, 5)
        s2m(4, 5)
        s2m(5, 5)
        s2m(6, 5)
        s2m(7, 0)
        ev(0, "S", 0, 1)
        s2m(7, 1)
        ev(1, "V", 0, 1)
        s2m(7, 2)
        ev(2, "S", 0, 1)
        s2m(7, 3)
        ev(3, "V", 0, 1)
        s2m(7, 4)
        ev(4, "S", 0, 1)
        s2m(7, 5)
        ev(5, "V", 0, 1)
        s2m(0, 6, 5)
        s2m(1, 6)
        s2m(2, 6)
        s2m(3, 6)
        s2m(4, 6)
        s2m(5, 6)
        s2m(6, 6)
        s2m(7, 6)
        ev(6, "S", 0, 1)
        s2m(0, 7, 6)
        s2m(1, 7)
        s2m(2, 7)
        s2m(3, 7)
        s2m(4, 7)
        s2m(5, 7)
        s2m(6, 7)
        s2m(7, 7)
        ev(7, "V", 0, 2)
        ev(7, "S", 1, 2)
